import numpy as np
import ml_dtypes


def mxq(x, axis, fmt="e4m3"):
    dtype, down = {"e4m3": (ml_dtypes.float8_e4m3fn, 7), "e5m2": (ml_dtypes.float8_e5m2, 14)}[fmt]
    v = np.moveaxis(np.asarray(x, np.float32).astype(ml_dtypes.bfloat16).astype(np.float64), axis, -1)
    blocks = v.reshape(v.shape[:-1] + (-1, 32))
    amax = np.abs(blocks).max(-1, keepdims=True)
    byte = np.maximum(np.where(amax > 0, np.frexp(amax)[1] - 1 + 127, 0) - down, 1)
    scale = np.exp2(byte - 127.0)
    codes = (blocks / scale).astype(np.float32).astype(dtype).astype(np.float64)
    return np.moveaxis((codes * scale).reshape(v.shape), -1, axis)


WIDE = False


def mx_kscale(k):
    if not WIDE:
        return np.ones(k)
    levels = np.array([10, -10, 5, -5, 0])
    a = np.random.permutation(np.resize(levels, k // 512 * 4)).reshape(k // 512, 4)
    idx = np.arange(k)
    return np.exp2(a[idx // 512, idx % 128 // 32])


BF16 = ml_dtypes.bfloat16


def bf(x):
    return np.asarray(x, np.float32).astype(BF16)


def f64(x):
    return np.asarray(x).astype(np.float64)


B, HEAD, NUM_EXPERTS, HEAD_DIM = 4096, 1, 3, 512
EPS = 1e-5
VAR0 = 3e-4


def setup_inputs():
    s = mx_kscale(HEAD_DIM)
    p = (HEAD, NUM_EXPERTS, HEAD_DIM)

    def draw_x():
        return bf((np.random.standard_normal((B, HEAD, HEAD_DIM)) * s).reshape(B, HEAD * HEAD_DIM))

    return {"x1": draw_x(), "x2": draw_x(), "x3": draw_x(),
            "W": bf(np.random.standard_normal((HEAD, NUM_EXPERTS, HEAD_DIM, HEAD_DIM)) / np.sqrt(HEAD_DIM) / s),
            "b": bf(np.random.standard_normal(p) * 0.3),
            "gamma": bf(np.sqrt(VAR0) * (1.0 + 0.1 * np.random.standard_normal(p))),
            "beta": bf(np.random.standard_normal(p) * 0.3),
            "running_mean": bf(np.random.standard_normal(p) * 0.3),
            "running_var": bf(VAR0 * np.random.uniform(0.5, 1.5, p))}


def reference(x1, x2, x3, W, b, gamma, beta, running_mean, running_var):
    n = x1.shape[0]
    xs = np.stack([f64(x1).reshape(n, HEAD, HEAD_DIM),
                   f64(x2).reshape(n, HEAD, HEAD_DIM),
                   f64(x3).reshape(n, HEAD, HEAD_DIM)], axis=2)
    xq = mxq(xs, 3, "e4m3")
    wq = mxq(f64(W), 3, "e4m3")
    y = (xq.transpose(1, 2, 0, 3) @ wq.transpose(0, 1, 3, 2)).transpose(2, 0, 1, 3) + f64(b)
    y = y * (1.0 / (1.0 + np.exp(-1.702 * y)))
    y = (y - f64(running_mean)) * (1.0 / np.sqrt(f64(running_var) + EPS)) * f64(gamma) + f64(beta)
    return np.transpose(y, (0, 2, 1, 3)).reshape(n, NUM_EXPERTS * HEAD * HEAD_DIM)

@@ -1,0 +1,216 @@
+from contextlib import ExitStack
+
+import concourse.mybir as mybir
+from concourse.masks import make_identity
+
+F32 = mybir.dt.float32
+BF16 = mybir.dt.bfloat16
+U32 = mybir.dt.uint32
+U8 = mybir.dt.uint8
+FP8X4 = mybir.dt.float8_e4m3fn_x4
+ACT = mybir.ActivationFunctionType
+ALU = mybir.AluOpType
+
+P = 128
+TOKENS = 4096
+D = 512
+E = 3
+EPS = 1e-5
+JT = TOKENS // P
+TB = 8
+NR = TB * E
+FLOPS = 2 * TOKENS * D * D * E
+
+X_BUFS = 20
+PREFETCH = 16
+
+
+def tile_mom_t_kernel(tc, x1, x2, x3, W, b, gamma, beta, running_mean, running_var, out):
+    nc = tc.nc
+    xs = [x.rearrange("(p j) k -> p (j k)", j=JT) for x in (x1, x2, x3)]
+    w_rows = W.rearrange("o e f k -> (o e f) k")
+    out_v = out.rearrange("(p j) c -> p j c", j=JT)
+
+    with ExitStack() as ctx:
+        const = ctx.enter_context(tc.tile_pool(name="const", bufs=1))
+        xin_pool = ctx.enter_context(tc.tile_pool(name="xin", bufs=X_BUFS))
+        grp_pool = ctx.enter_context(tc.tile_pool(name="grp", bufs=3))
+        q_pool = ctx.enter_context(tc.tile_pool(name="q", bufs=3))
+        z_pool = ctx.enter_context(tc.tile_pool(name="z", bufs=3))
+        st_pool = ctx.enter_context(tc.tile_pool(name="st", bufs=3))
+        psum = ctx.enter_context(tc.psum_pool(name="psum", bufs=8))
+        ctx.enter_context(tc.manual_schedule())
+
+        ident = const.tile([P, P], F32, name="ident")
+        make_identity(nc, ident[:])
+
+        prow = const.tile([P, P], BF16, name="prow")
+        nc.vector.memset(prow[:], 0.0)
+        for i, v in enumerate((b, gamma, beta, running_mean, running_var)):
+            nc.scalar.dma_start(out=prow[16 * i : 16 * i + 12, :], in_=v.rearrange("o e (q c) -> (o e q) c", c=P))
+
+        xin = {}
+        win = {}
+
+        def load_w(e):
+            t = xin_pool.tile([P, 4 * D], BF16, name="win%d" % e, tag="xin")
+            nc.sync.dma_start(
+                out=t[:].rearrange("p (q k) -> p q k", q=4),
+                in_=w_rows[e * D : (e + 1) * D, :].rearrange("(q p) k -> p q k", p=P),
+            )
+            win[e] = t
+
+        def load_x(r):
+            tb, e = divmod(r, E)
+            t = xin_pool.tile([P, 4 * D], BF16, name="xin%d" % r, tag="xin")
+            nc.sync.dma_start(out=t[:], in_=xs[e][:, tb * 4 * D : (tb + 1) * 4 * D])
+            xin[r] = t
+
+        for e in range(E):
+            load_w(e)
+            load_x(e)
+        for r in range(E, PREFETCH):
+            load_x(r)
+
+        w_codes = [const.tile([P, D], U32, name="wc%d" % e, align_bytes=64) for e in range(E)]
+        w_scales = [const.tile([P, D], U8, name="ws%d" % e, align_bytes=64) for e in range(E)]
+        grouped = {}
+        codes = {}
+        scales = {}
+        zt = {}
+        stage = {}
+        par = {}
+
+        def transposes_in(src, key, on_scalar):
+            sf = src[:].bitcast(F32)
+            g = grp_pool.tile([P, 4 * D], BF16, name="g_%s" % key, tag="g", align_bytes=64)
+            gf = g[:].bitcast(F32)
+            banks = []
+            for h in range(2):
+                bank = psum.tile([P, D], F32, name="a_%s_%d" % (key, h), tag="bank")
+                for jj in (2 * h, 2 * h + 1):
+                    for u in range(2):
+                        nc.tensor.transpose(
+                            bank[:, u * 256 + (jj % 2) * P : u * 256 + (jj % 2) * P + P],
+                            sf[:, jj * 256 + u * P : jj * 256 + u * P + P],
+                            ident[:],
+                        )
+                banks.append(bank)
+            for h in range(2):
+                dst = gf[:, h * D : (h + 1) * D].rearrange("p (c u) -> p c u", u=2)
+                srcv = banks[h][:].rearrange("p (u c) -> p c u", u=2)
+                if h == 1 and on_scalar:
+                    nc.scalar.copy(out=dst, in_=srcv)
+                else:
+                    nc.vector.tensor_copy(out=dst, in_=srcv)
+            return g
+
+        def params():
+            pf = const.tile([P, P], F32, name="pf")
+            nc.vector.tensor_copy(out=pf[:], in_=prow[:])
+            bank = psum.tile([P, D], F32, name="pbank", tag="bank")
+            nc.tensor.transpose(bank[:, 0:P], pf[:], ident[:])
+            pt = const.tile([P, P], F32, name="pt")
+            nc.vector.tensor_copy(out=pt[:], in_=bank[:, 0:P])
+            sd = const.tile([P, 12], F32, name="sd")
+            nc.vector.tensor_scalar_add(out=sd[:], in0=pt[:, 64:76], scalar1=EPS)
+            nc.scalar.activation(out=sd[:], in_=sd[:], func=ACT.Sqrt)
+            s_t = const.tile([P, 12], F32, name="s_t")
+            nc.vector.reciprocal(out=s_t[:], in_=sd[:])
+            nc.vector.tensor_mul(out=s_t[:], in0=s_t[:], in1=pt[:, 16:28])
+            t_t = const.tile([P, 12], F32, name="t_t")
+            nc.vector.tensor_mul(out=t_t[:], in0=pt[:, 48:60], in1=s_t[:])
+            nc.vector.tensor_sub(out=t_t[:], in0=pt[:, 32:44], in1=t_t[:])
+            par["b"] = pt
+            par["s"] = s_t
+            par["t"] = t_t
+
+        def store(tb, lo, hi, c0, c1):
+            nc.sync.dma_start(
+                out=out_v[:, tb * 4 + lo : tb * 4 + hi, c0:c1],
+                in_=stage[tb][:].rearrange("p (j c) -> p j c", j=4)[:, lo:hi, c0:c1],
+            )
+
+        for s in range(-2, NR + 1):
+            if 0 <= s < NR:
+                e = s % E
+                z = z_pool.tile([P, 4, D], F32, name="z%d" % s, tag="z")
+                zt[s] = z
+                accs = []
+                for fb in range(4):
+                    acc = psum.tile([P, D], F32, name="acc%d_%d" % (s, fb), tag="bank")
+                    nc.tensor.matmul_mx(
+                        out=acc[:],
+                        lhsT=w_codes[e][:, fb * P : (fb + 1) * P].bitcast(FP8X4),
+                        lhsT_scale=w_scales[e][:, fb * P : (fb + 1) * P],
+                        rhs=codes[s][:].bitcast(FP8X4),
+                        rhs_scale=scales[s][:],
+                        start=True,
+                        stop=True,
+                    )
+                    accs.append(acc)
+                for fb in range(4):
+                    col = e * 4 + fb
+                    nc.scalar.activation(
+                        out=z[:, fb, :], in_=accs[fb][:], func=ACT.Gelu_apprx_sigmoid,
+                        bias=par["b"][:, col : col + 1], scale=1.0,
+                    )
+                for fb in range(4):
+                    col = e * 4 + fb
+                    nc.gpsimd.tensor_scalar(
+                        out=z[:, fb, :], in0=z[:, fb, :],
+                        scalar1=par["s"][:, col : col + 1], scalar2=par["t"][:, col : col + 1],
+                        op0=ALU.mult, op1=ALU.add,
+                    )
+            q = s + 1
+            if 0 <= q < E:
+                nc.vector.quantize_mx(out=w_codes[q][:].bitcast(FP8X4), scales=w_scales[q][:], in_=grouped["w%d" % q][:])
+            if 0 <= q < NR:
+                c_t = q_pool.tile([P, D], U32, name="c%d" % q, tag="c", align_bytes=64)
+                s_t2 = q_pool.tile([P, D], U8, name="s%d" % q, tag="s", align_bytes=64)
+                nc.vector.quantize_mx(out=c_t[:].bitcast(FP8X4), scales=s_t2[:], in_=grouped[q][:])
+                codes[q] = c_t
+                scales[q] = s_t2
+            a = s + 2
+            if 0 <= a < E:
+                grouped["w%d" % a] = transposes_in(win[a], "w%d" % a, True)
+            if 0 <= a < NR:
+                grouped[a] = transposes_in(xin[a], "x%d" % a, a < 3)
+            if s == -2:
+                params()
+            o = s - 1
+            if 0 <= o < NR:
+                tb, e = divmod(o, E)
+                if e == 0:
+                    stage[tb] = st_pool.tile([P, 4 * E * D], F32, name="st%d" % tb, tag="st")
+                banks = []
+                for jj in range(4):
+                    bank = psum.tile([P, D], F32, name="o%d_%d" % (o, jj), tag="bank")
+                    for fb in range(4):
+                        nc.tensor.transpose(bank[:, fb * P : (fb + 1) * P], zt[o][:, fb, jj * P : (jj + 1) * P], ident[:])
+                    banks.append(bank)
+                if o == NR - 1:
+                    on_scalar = (0, 2)
+                elif o % 2 == 1:
+                    on_scalar = (0, 1)
+                else:
+                    on_scalar = (0,)
+                for jj in range(4):
+                    dst = stage[tb][:, jj * E * D + e * D : jj * E * D + (e + 1) * D]
+                    if jj in on_scalar:
+                        nc.scalar.copy(out=dst, in_=banks[jj][:])
+                    else:
+                        nc.vector.tensor_copy(out=dst, in_=banks[jj][:])
+            ld = s + PREFETCH
+            if PREFETCH <= ld < NR:
+                load_x(ld)
+            if 0 <= o < NR:
+                tb, e = divmod(o, E)
+                if tb < TB - 1:
+                    if e == E - 1:
+                        store(tb, 0, 4, 0, E * D)
+                elif e == 1:
+                    store(tb, 0, 4, 0, 2 * D)
+                elif e == 2:
+                    store(tb, 0, 2, 2 * D, 3 * D)
+                    store(tb, 2, 4, 2 * D, 3 * D)

@@ -23,6 +23,7 @@ FLOPS = 2 * TOKENS * D * D * E
 
 X_BUFS = 20
 PREFETCH = 16
+LAG = 2
 
 
 def tile_mom_t_kernel(tc, x1, x2, x3, W, b, gamma, beta, running_mean, running_var, out):
@@ -36,10 +37,17 @@ def tile_mom_t_kernel(tc, x1, x2, x3, W, b, gamma, beta, running_mean, running_v
         xin_pool = ctx.enter_context(tc.tile_pool(name="xin", bufs=X_BUFS))
         grp_pool = ctx.enter_context(tc.tile_pool(name="grp", bufs=3))
         q_pool = ctx.enter_context(tc.tile_pool(name="q", bufs=3))
-        z_pool = ctx.enter_context(tc.tile_pool(name="z", bufs=3))
+        z_pool = ctx.enter_context(tc.tile_pool(name="z", bufs=LAG + 2))
         st_pool = ctx.enter_context(tc.tile_pool(name="st", bufs=3))
-        psum = ctx.enter_context(tc.psum_pool(name="psum", bufs=8))
+        psum = ctx.enter_context(tc.psum_pool(name="psum", bufs=1))
         ctx.enter_context(tc.manual_schedule())
+
+        jobs = [0]
+
+        def next_bank():
+            n = jobs[0]
+            jobs[0] = n + 1
+            return psum.tile([P, D], F32, name="bank_job%d" % n, tag="bank%d" % (n % 8))
 
         ident = const.tile([P, P], F32, name="ident")
         make_identity(nc, ident[:])
@@ -81,13 +89,13 @@ def tile_mom_t_kernel(tc, x1, x2, x3, W, b, gamma, beta, running_mean, running_v
         stage = {}
         par = {}
 
-        def transposes_in(src, key, on_scalar):
+        def transposes_in(src, key):
             sf = src[:].bitcast(F32)
             g = grp_pool.tile([P, 4 * D], BF16, name="g_%s" % key, tag="g", align_bytes=64)
             gf = g[:].bitcast(F32)
             banks = []
             for h in range(2):
-                bank = psum.tile([P, D], F32, name="a_%s_%d" % (key, h), tag="bank")
+                bank = next_bank()
                 for jj in (2 * h, 2 * h + 1):
                     for u in range(2):
                         nc.tensor.transpose(
@@ -99,7 +107,7 @@ def tile_mom_t_kernel(tc, x1, x2, x3, W, b, gamma, beta, running_mean, running_v
             for h in range(2):
                 dst = gf[:, h * D : (h + 1) * D].rearrange("p (c u) -> p c u", u=2)
                 srcv = banks[h][:].rearrange("p (u c) -> p c u", u=2)
-                if h == 1 and on_scalar:
+                if h == 1:
                     nc.scalar.copy(out=dst, in_=srcv)
                 else:
                     nc.vector.tensor_copy(out=dst, in_=srcv)
@@ -108,7 +116,7 @@ def tile_mom_t_kernel(tc, x1, x2, x3, W, b, gamma, beta, running_mean, running_v
         def params():
             pf = const.tile([P, P], F32, name="pf")
             nc.vector.tensor_copy(out=pf[:], in_=prow[:])
-            bank = psum.tile([P, D], F32, name="pbank", tag="bank")
+            bank = next_bank()
             nc.tensor.transpose(bank[:, 0:P], pf[:], ident[:])
             pt = const.tile([P, P], F32, name="pt")
             nc.vector.tensor_copy(out=pt[:], in_=bank[:, 0:P])
@@ -131,37 +139,70 @@ def tile_mom_t_kernel(tc, x1, x2, x3, W, b, gamma, beta, running_mean, running_v
                 in_=stage[tb][:].rearrange("p (j c) -> p j c", j=4)[:, lo:hi, c0:c1],
             )
 
-        for s in range(-2, NR + 1):
-            if 0 <= s < NR:
-                e = s % E
-                z = z_pool.tile([P, 4, D], F32, name="z%d" % s, tag="z")
-                zt[s] = z
-                accs = []
+        def affine(eng, s, fb):
+            col = (s % E) * 4 + fb
+            eng.tensor_scalar(
+                out=zt[s][:, fb, :], in0=zt[s][:, fb, :],
+                scalar1=par["s"][:, col : col + 1], scalar2=par["t"][:, col : col + 1],
+                op0=ALU.mult, op1=ALU.add,
+            )
+
+        def mx_pair(s, fbs):
+            e = s % E
+            accs = []
+            for fb in fbs:
+                acc = next_bank()
+                nc.tensor.matmul_mx(
+                    out=acc[:],
+                    lhsT=w_codes[e][:, fb * P : (fb + 1) * P].bitcast(FP8X4),
+                    lhsT_scale=w_scales[e][:, fb * P : (fb + 1) * P],
+                    rhs=codes[s][:].bitcast(FP8X4),
+                    rhs_scale=scales[s][:],
+                    start=True,
+                    stop=True,
+                )
+                accs.append(acc)
+            for fb, acc in zip(fbs, accs):
+                col = e * 4 + fb
+                nc.scalar.activation(
+                    out=zt[s][:, fb, :], in_=acc[:], func=ACT.Gelu_apprx_sigmoid,
+                    bias=par["b"][:, col : col + 1], scale=1.0,
+                )
+            if s < NR - 1 or fbs[0] == 0:
+                for fb in fbs:
+                    affine(nc.gpsimd, s, fb)
+
+        def back(o, jjs, on_scalar):
+            tb, e = divmod(o, E)
+            banks = []
+            for jj in jjs:
+                bank = next_bank()
                 for fb in range(4):
-                    acc = psum.tile([P, D], F32, name="acc%d_%d" % (s, fb), tag="bank")
-                    nc.tensor.matmul_mx(
-                        out=acc[:],
-                        lhsT=w_codes[e][:, fb * P : (fb + 1) * P].bitcast(FP8X4),
-                        lhsT_scale=w_scales[e][:, fb * P : (fb + 1) * P],
-                        rhs=codes[s][:].bitcast(FP8X4),
-                        rhs_scale=scales[s][:],
-                        start=True,
-                        stop=True,
-                    )
-                    accs.append(acc)
-                for fb in range(4):
-                    col = e * 4 + fb
-                    nc.scalar.activation(
-                        out=z[:, fb, :], in_=accs[fb][:], func=ACT.Gelu_apprx_sigmoid,
-                        bias=par["b"][:, col : col + 1], scale=1.0,
-                    )
-                for fb in range(4):
-                    col = e * 4 + fb
-                    nc.gpsimd.tensor_scalar(
-                        out=z[:, fb, :], in0=z[:, fb, :],
-                        scalar1=par["s"][:, col : col + 1], scalar2=par["t"][:, col : col + 1],
-                        op0=ALU.mult, op1=ALU.add,
-                    )
+                    nc.tensor.transpose(bank[:, fb * P : (fb + 1) * P], zt[o][:, fb, jj * P : (jj + 1) * P], ident[:])
+                banks.append(bank)
+            for jj, bank in zip(jjs, banks):
+                dst = stage[tb][:, jj * E * D + e * D : jj * E * D + (e + 1) * D]
+                if jj in on_scalar:
+                    nc.scalar.copy(out=dst, in_=bank[:])
+                else:
+                    nc.vector.tensor_copy(out=dst, in_=bank[:])
+
+        for s in range(-2, NR + LAG):
+            o = s - LAG
+            has_mx = 0 <= s < NR
+            has_back = 0 <= o < NR
+            if has_back and o % E == 0:
+                stage[o // E] = st_pool.tile([P, 4 * E * D], F32, name="st%d" % (o // E), tag="st")
+            if o == NR - 1:
+                on_scalar = (0, 2)
+            elif o % 2 == 1:
+                on_scalar = (1,)
+            else:
+                on_scalar = ()
+
+            if has_mx:
+                zt[s] = z_pool.tile([P, 4, D], F32, name="z%d" % s, tag="z")
+                mx_pair(s, (0, 1))
             q = s + 1
             if 0 <= q < E:
                 nc.vector.quantize_mx(out=w_codes[q][:].bitcast(FP8X4), scales=w_scales[q][:], in_=grouped["w%d" % q][:])
@@ -173,38 +214,25 @@ def tile_mom_t_kernel(tc, x1, x2, x3, W, b, gamma, beta, running_mean, running_v
                 scales[q] = s_t2
             a = s + 2
             if 0 <= a < E:
-                grouped["w%d" % a] = transposes_in(win[a], "w%d" % a, True)
+                grouped["w%d" % a] = transposes_in(win[a], "w%d" % a)
             if 0 <= a < NR:
-                grouped[a] = transposes_in(xin[a], "x%d" % a, a < 3)
+                grouped[a] = transposes_in(xin[a], "x%d" % a)
             if s == -2:
                 params()
-            o = s - 1
-            if 0 <= o < NR:
-                tb, e = divmod(o, E)
-                if e == 0:
-                    stage[tb] = st_pool.tile([P, 4 * E * D], F32, name="st%d" % tb, tag="st")
-                banks = []
-                for jj in range(4):
-                    bank = psum.tile([P, D], F32, name="o%d_%d" % (o, jj), tag="bank")
-                    for fb in range(4):
-                        nc.tensor.transpose(bank[:, fb * P : (fb + 1) * P], zt[o][:, fb, jj * P : (jj + 1) * P], ident[:])
-                    banks.append(bank)
-                if o == NR - 1:
-                    on_scalar = (0, 2)
-                elif o % 2 == 1:
-                    on_scalar = (0, 1)
-                else:
-                    on_scalar = (0,)
-                for jj in range(4):
-                    dst = stage[tb][:, jj * E * D + e * D : jj * E * D + (e + 1) * D]
-                    if jj in on_scalar:
-                        nc.scalar.copy(out=dst, in_=banks[jj][:])
-                    else:
-                        nc.vector.tensor_copy(out=dst, in_=banks[jj][:])
+            if has_back:
+                back(o, (0,), on_scalar)
+            if has_mx:
+                mx_pair(s, (2, 3))
+            if has_back:
+                back(o, (1, 2, 3), on_scalar)
+            if s == NR - 1:
+                affine(nc.vector, s, 2)
+                affine(nc.vector, s, 3)
+
             ld = s + PREFETCH
             if PREFETCH <= ld < NR:
                 load_x(ld)
-            if 0 <= o < NR:
+            if has_back:
                 tb, e = divmod(o, E)
                 if tb < TB - 1:
                     if e == E - 1:

@@ -44,10 +44,10 @@ def tile_mom_t_kernel(tc, x1, x2, x3, W, b, gamma, beta, running_mean, running_v
 
         jobs = [0]
 
-        def next_bank():
+        def next_pair():
             n = jobs[0]
             jobs[0] = n + 1
-            return psum.tile([P, D], F32, name="bank_job%d" % n, tag="bank%d" % (n % 8))
+            return psum.tile([P, 2, D], F32, name="pair_job%d" % n, tag="pair%d" % (n % 4))
 
         ident = const.tile([P, P], F32, name="ident")
         make_identity(nc, ident[:])
@@ -62,16 +62,20 @@ def tile_mom_t_kernel(tc, x1, x2, x3, W, b, gamma, beta, running_mean, running_v
 
         def load_w(e):
             t = xin_pool.tile([P, 4 * D], BF16, name="win%d" % e, tag="xin")
-            nc.sync.dma_start(
-                out=t[:].rearrange("p (q k) -> p q k", q=4),
-                in_=w_rows[e * D : (e + 1) * D, :].rearrange("(q p) k -> p q k", p=P),
-            )
+            cuts = (0, 2, 4) if e == 0 else (0, 4)
+            for lo, hi in zip(cuts[:-1], cuts[1:]):
+                nc.sync.dma_start(
+                    out=t[:].rearrange("p (q k) -> p q k", q=4)[:, lo:hi, :],
+                    in_=w_rows[e * D + lo * P : e * D + hi * P, :].rearrange("(q p) k -> p q k", p=P),
+                )
             win[e] = t
 
         def load_x(r):
             tb, e = divmod(r, E)
             t = xin_pool.tile([P, 4 * D], BF16, name="xin%d" % r, tag="xin")
-            nc.sync.dma_start(out=t[:], in_=xs[e][:, tb * 4 * D : (tb + 1) * 4 * D])
+            cuts = (0, 2, 4) if r == 0 else (0, 4)
+            for lo, hi in zip(cuts[:-1], cuts[1:]):
+                nc.sync.dma_start(out=t[:, lo * D : hi * D], in_=xs[e][:, (tb * 4 + lo) * D : (tb * 4 + hi) * D])
             xin[r] = t
 
         for e in range(E):
@@ -89,25 +93,23 @@ def tile_mom_t_kernel(tc, x1, x2, x3, W, b, gamma, beta, running_mean, running_v
         stage = {}
         par = {}
 
-        def transposes_in(src, key):
+        def transposes_in(src, key, on_scalar):
             sf = src[:].bitcast(F32)
             g = grp_pool.tile([P, 4 * D], BF16, name="g_%s" % key, tag="g", align_bytes=64)
             gf = g[:].bitcast(F32)
-            banks = []
+            pair = next_pair()
             for h in range(2):
-                bank = next_bank()
                 for jj in (2 * h, 2 * h + 1):
                     for u in range(2):
                         nc.tensor.transpose(
-                            bank[:, u * 256 + (jj % 2) * P : u * 256 + (jj % 2) * P + P],
+                            pair[:, h, u * 256 + (jj % 2) * P : u * 256 + (jj % 2) * P + P],
                             sf[:, jj * 256 + u * P : jj * 256 + u * P + P],
                             ident[:],
                         )
-                banks.append(bank)
             for h in range(2):
                 dst = gf[:, h * D : (h + 1) * D].rearrange("p (c u) -> p c u", u=2)
-                srcv = banks[h][:].rearrange("p (u c) -> p c u", u=2)
-                if h == 1:
+                srcv = pair[:, h, :].rearrange("p (u c) -> p c u", u=2)
+                if h == 1 and on_scalar:
                     nc.scalar.copy(out=dst, in_=srcv)
                 else:
                     nc.vector.tensor_copy(out=dst, in_=srcv)
@@ -116,10 +118,10 @@ def tile_mom_t_kernel(tc, x1, x2, x3, W, b, gamma, beta, running_mean, running_v
         def params():
             pf = const.tile([P, P], F32, name="pf")
             nc.vector.tensor_copy(out=pf[:], in_=prow[:])
-            bank = next_bank()
-            nc.tensor.transpose(bank[:, 0:P], pf[:], ident[:])
+            pair = next_pair()
+            nc.tensor.transpose(pair[:, 0, 0:P], pf[:], ident[:])
             pt = const.tile([P, P], F32, name="pt")
-            nc.vector.tensor_copy(out=pt[:], in_=bank[:, 0:P])
+            nc.vector.tensor_copy(out=pt[:], in_=pair[:, 0, 0:P])
             sd = const.tile([P, 12], F32, name="sd")
             nc.vector.tensor_scalar_add(out=sd[:], in0=pt[:, 64:76], scalar1=EPS)
             nc.scalar.activation(out=sd[:], in_=sd[:], func=ACT.Sqrt)
@@ -147,45 +149,49 @@ def tile_mom_t_kernel(tc, x1, x2, x3, W, b, gamma, beta, running_mean, running_v
                 op0=ALU.mult, op1=ALU.add,
             )
 
-        def mx_pair(s, fbs):
+        def mx_round(s):
             e = s % E
             accs = []
-            for fb in fbs:
-                acc = next_bank()
-                nc.tensor.matmul_mx(
-                    out=acc[:],
-                    lhsT=w_codes[e][:, fb * P : (fb + 1) * P].bitcast(FP8X4),
-                    lhsT_scale=w_scales[e][:, fb * P : (fb + 1) * P],
-                    rhs=codes[s][:].bitcast(FP8X4),
-                    rhs_scale=scales[s][:],
-                    start=True,
-                    stop=True,
-                )
-                accs.append(acc)
-            for fb, acc in zip(fbs, accs):
+            for half in range(2):
+                pair = next_pair()
+                for fb in (2 * half, 2 * half + 1):
+                    acc = pair[:, fb % 2, :]
+                    nc.tensor.matmul_mx(
+                        out=acc,
+                        lhsT=w_codes[e][:, fb * P : (fb + 1) * P].bitcast(FP8X4),
+                        lhsT_scale=w_scales[e][:, fb * P : (fb + 1) * P],
+                        rhs=codes[s][:].bitcast(FP8X4),
+                        rhs_scale=scales[s][:],
+                        start=True,
+                        stop=True,
+                    )
+                    accs.append(acc)
+            for fb in range(4):
                 col = e * 4 + fb
                 nc.scalar.activation(
-                    out=zt[s][:, fb, :], in_=acc[:], func=ACT.Gelu_apprx_sigmoid,
+                    out=zt[s][:, fb, :], in_=accs[fb], func=ACT.Gelu_apprx_sigmoid,
                     bias=par["b"][:, col : col + 1], scale=1.0,
                 )
-            if s < NR - 1 or fbs[0] == 0:
-                for fb in fbs:
+            for fb in range(4):
+                if s < NR - 1 or fb < 2:
                     affine(nc.gpsimd, s, fb)
 
-        def back(o, jjs, on_scalar):
+        def back(o, jjs):
             tb, e = divmod(o, E)
-            banks = []
+            pair = next_pair()
             for jj in jjs:
-                bank = next_bank()
                 for fb in range(4):
-                    nc.tensor.transpose(bank[:, fb * P : (fb + 1) * P], zt[o][:, fb, jj * P : (jj + 1) * P], ident[:])
-                banks.append(bank)
-            for jj, bank in zip(jjs, banks):
+                    nc.tensor.transpose(pair[:, jj % 2, fb * P : (fb + 1) * P], zt[o][:, fb, jj * P : (jj + 1) * P], ident[:])
+            return pair
+
+        def back_out(o, jjs, pair, on_scalar):
+            tb, e = divmod(o, E)
+            for jj in jjs:
                 dst = stage[tb][:, jj * E * D + e * D : jj * E * D + (e + 1) * D]
                 if jj in on_scalar:
-                    nc.scalar.copy(out=dst, in_=bank[:])
+                    nc.scalar.copy(out=dst, in_=pair[:, jj % 2, :])
                 else:
-                    nc.vector.tensor_copy(out=dst, in_=bank[:])
+                    nc.vector.tensor_copy(out=dst, in_=pair[:, jj % 2, :])
 
         for s in range(-2, NR + LAG):
             o = s - LAG
@@ -196,13 +202,13 @@ def tile_mom_t_kernel(tc, x1, x2, x3, W, b, gamma, beta, running_mean, running_v
             if o == NR - 1:
                 on_scalar = (0, 2)
             elif o % 2 == 1:
-                on_scalar = (1,)
+                on_scalar = (0, 1)
             else:
-                on_scalar = ()
+                on_scalar = (0,)
 
             if has_mx:
                 zt[s] = z_pool.tile([P, 4, D], F32, name="z%d" % s, tag="z")
-                mx_pair(s, (0, 1))
+                mx_round(s)
             q = s + 1
             if 0 <= q < E:
                 nc.vector.quantize_mx(out=w_codes[q][:].bitcast(FP8X4), scales=w_scales[q][:], in_=grouped["w%d" % q][:])
@@ -214,17 +220,16 @@ def tile_mom_t_kernel(tc, x1, x2, x3, W, b, gamma, beta, running_mean, running_v
                 scales[q] = s_t2
             a = s + 2
             if 0 <= a < E:
-                grouped["w%d" % a] = transposes_in(win[a], "w%d" % a)
+                grouped["w%d" % a] = transposes_in(win[a], "w%d" % a, True)
             if 0 <= a < NR:
-                grouped[a] = transposes_in(xin[a], "x%d" % a)
+                grouped[a] = transposes_in(xin[a], "x%d" % a, a < E)
             if s == -2:
                 params()
             if has_back:
-                back(o, (0,), on_scalar)
-            if has_mx:
-                mx_pair(s, (2, 3))
-            if has_back:
-                back(o, (1, 2, 3), on_scalar)
+                pair_a = back(o, (0, 1))
+                pair_b = back(o, (2, 3))
+                back_out(o, (0, 1), pair_a, on_scalar)
+                back_out(o, (2, 3), pair_b, on_scalar)
             if s == NR - 1:
                 affine(nc.vector, s, 2)
                 affine(nc.vector, s, 3)

@@ -23,7 +23,6 @@ FLOPS = 2 * TOKENS * D * D * E
 
 X_BUFS = 20
 PREFETCH = 16
-LAG = 2
 
 
 def tile_mom_t_kernel(tc, x1, x2, x3, W, b, gamma, beta, running_mean, running_var, out):
@@ -37,17 +36,10 @@ def tile_mom_t_kernel(tc, x1, x2, x3, W, b, gamma, beta, running_mean, running_v
         xin_pool = ctx.enter_context(tc.tile_pool(name="xin", bufs=X_BUFS))
         grp_pool = ctx.enter_context(tc.tile_pool(name="grp", bufs=3))
         q_pool = ctx.enter_context(tc.tile_pool(name="q", bufs=3))
-        z_pool = ctx.enter_context(tc.tile_pool(name="z", bufs=LAG + 2))
+        z_pool = ctx.enter_context(tc.tile_pool(name="z", bufs=3))
         st_pool = ctx.enter_context(tc.tile_pool(name="st", bufs=3))
-        psum = ctx.enter_context(tc.psum_pool(name="psum", bufs=1))
+        psum = ctx.enter_context(tc.psum_pool(name="psum", bufs=8))
         ctx.enter_context(tc.manual_schedule())
-
-        jobs = [0]
-
-        def next_pair():
-            n = jobs[0]
-            jobs[0] = n + 1
-            return psum.tile([P, 2, D], F32, name="pair_job%d" % n, tag="pair%d" % (n % 4))
 
         ident = const.tile([P, P], F32, name="ident")
         make_identity(nc, ident[:])
@@ -62,7 +54,7 @@ def tile_mom_t_kernel(tc, x1, x2, x3, W, b, gamma, beta, running_mean, running_v
 
         def load_w(e):
             t = xin_pool.tile([P, 4 * D], BF16, name="win%d" % e, tag="xin")
-            cuts = (0, 2, 4) if e == 0 else (0, 4)
+            cuts = (0, 1, 2, 4) if e == 0 else (0, 4)
             for lo, hi in zip(cuts[:-1], cuts[1:]):
                 nc.sync.dma_start(
                     out=t[:].rearrange("p (q k) -> p q k", q=4)[:, lo:hi, :],
@@ -97,41 +89,50 @@ def tile_mom_t_kernel(tc, x1, x2, x3, W, b, gamma, beta, running_mean, running_v
             sf = src[:].bitcast(F32)
             g = grp_pool.tile([P, 4 * D], BF16, name="g_%s" % key, tag="g", align_bytes=64)
             gf = g[:].bitcast(F32)
-            pair = next_pair()
+            banks = []
             for h in range(2):
+                bank = psum.tile([P, D], F32, name="a_%s_%d" % (key, h), tag="bank")
                 for jj in (2 * h, 2 * h + 1):
                     for u in range(2):
                         nc.tensor.transpose(
-                            pair[:, h, u * 256 + (jj % 2) * P : u * 256 + (jj % 2) * P + P],
+                            bank[:, u * 256 + (jj % 2) * P : u * 256 + (jj % 2) * P + P],
                             sf[:, jj * 256 + u * P : jj * 256 + u * P + P],
                             ident[:],
                         )
+                banks.append(bank)
             for h in range(2):
                 dst = gf[:, h * D : (h + 1) * D].rearrange("p (c u) -> p c u", u=2)
-                srcv = pair[:, h, :].rearrange("p (u c) -> p c u", u=2)
+                srcv = banks[h][:].rearrange("p (u c) -> p c u", u=2)
                 if h == 1 and on_scalar:
                     nc.scalar.copy(out=dst, in_=srcv)
                 else:
                     nc.vector.tensor_copy(out=dst, in_=srcv)
             return g
 
-        def params():
+        def params_transpose():
             pf = const.tile([P, P], F32, name="pf")
             nc.vector.tensor_copy(out=pf[:], in_=prow[:])
-            pair = next_pair()
-            nc.tensor.transpose(pair[:, 0, 0:P], pf[:], ident[:])
+            bank = psum.tile([P, D], F32, name="pbank", tag="bank")
+            nc.tensor.transpose(bank[:, 0:P], pf[:], ident[:])
+            par["bank"] = bank
+
+        def params_sqrt():
             pt = const.tile([P, P], F32, name="pt")
-            nc.vector.tensor_copy(out=pt[:], in_=pair[:, 0, 0:P])
+            nc.vector.tensor_copy(out=pt[:], in_=par["bank"][:, 0:P])
             sd = const.tile([P, 12], F32, name="sd")
             nc.vector.tensor_scalar_add(out=sd[:], in0=pt[:, 64:76], scalar1=EPS)
             nc.scalar.activation(out=sd[:], in_=sd[:], func=ACT.Sqrt)
+            par["b"] = pt
+            par["sd"] = sd
+
+        def params_affine():
+            pt = par["b"]
             s_t = const.tile([P, 12], F32, name="s_t")
-            nc.vector.reciprocal(out=s_t[:], in_=sd[:])
+            nc.vector.reciprocal(out=s_t[:], in_=par["sd"][:])
             nc.vector.tensor_mul(out=s_t[:], in0=s_t[:], in1=pt[:, 16:28])
             t_t = const.tile([P, 12], F32, name="t_t")
             nc.vector.tensor_mul(out=t_t[:], in0=pt[:, 48:60], in1=s_t[:])
             nc.vector.tensor_sub(out=t_t[:], in0=pt[:, 32:44], in1=t_t[:])
-            par["b"] = pt
             par["s"] = s_t
             par["t"] = t_t
 
@@ -141,23 +142,16 @@ def tile_mom_t_kernel(tc, x1, x2, x3, W, b, gamma, beta, running_mean, running_v
                 in_=stage[tb][:].rearrange("p (j c) -> p j c", j=4)[:, lo:hi, c0:c1],
             )
 
-        def affine(eng, s, fb):
-            col = (s % E) * 4 + fb
-            eng.tensor_scalar(
-                out=zt[s][:, fb, :], in0=zt[s][:, fb, :],
-                scalar1=par["s"][:, col : col + 1], scalar2=par["t"][:, col : col + 1],
-                op0=ALU.mult, op1=ALU.add,
-            )
-
-        def mx_round(s):
-            e = s % E
-            accs = []
-            for half in range(2):
-                pair = next_pair()
-                for fb in (2 * half, 2 * half + 1):
-                    acc = pair[:, fb % 2, :]
+        for s in range(-2, NR + 1):
+            if 0 <= s < NR:
+                e = s % E
+                z = z_pool.tile([P, 4, D], F32, name="z%d" % s, tag="z")
+                zt[s] = z
+                accs = []
+                for fb in range(4):
+                    acc = psum.tile([P, D], F32, name="acc%d_%d" % (s, fb), tag="bank")
                     nc.tensor.matmul_mx(
-                        out=acc,
+                        out=acc[:],
                         lhsT=w_codes[e][:, fb * P : (fb + 1) * P].bitcast(FP8X4),
                         lhsT_scale=w_scales[e][:, fb * P : (fb + 1) * P],
                         rhs=codes[s][:].bitcast(FP8X4),
@@ -166,49 +160,20 @@ def tile_mom_t_kernel(tc, x1, x2, x3, W, b, gamma, beta, running_mean, running_v
                         stop=True,
                     )
                     accs.append(acc)
-            for fb in range(4):
-                col = e * 4 + fb
-                nc.scalar.activation(
-                    out=zt[s][:, fb, :], in_=accs[fb], func=ACT.Gelu_apprx_sigmoid,
-                    bias=par["b"][:, col : col + 1], scale=1.0,
-                )
-            for fb in range(4):
-                if s < NR - 1 or fb < 2:
-                    affine(nc.gpsimd, s, fb)
-
-        def back(o, jjs):
-            tb, e = divmod(o, E)
-            pair = next_pair()
-            for jj in jjs:
                 for fb in range(4):
-                    nc.tensor.transpose(pair[:, jj % 2, fb * P : (fb + 1) * P], zt[o][:, fb, jj * P : (jj + 1) * P], ident[:])
-            return pair
-
-        def back_out(o, jjs, pair, on_scalar):
-            tb, e = divmod(o, E)
-            for jj in jjs:
-                dst = stage[tb][:, jj * E * D + e * D : jj * E * D + (e + 1) * D]
-                if jj in on_scalar:
-                    nc.scalar.copy(out=dst, in_=pair[:, jj % 2, :])
-                else:
-                    nc.vector.tensor_copy(out=dst, in_=pair[:, jj % 2, :])
-
-        for s in range(-2, NR + LAG):
-            o = s - LAG
-            has_mx = 0 <= s < NR
-            has_back = 0 <= o < NR
-            if has_back and o % E == 0:
-                stage[o // E] = st_pool.tile([P, 4 * E * D], F32, name="st%d" % (o // E), tag="st")
-            if o == NR - 1:
-                on_scalar = (0, 2)
-            elif o % 2 == 1:
-                on_scalar = (0, 1)
-            else:
-                on_scalar = (0,)
-
-            if has_mx:
-                zt[s] = z_pool.tile([P, 4, D], F32, name="z%d" % s, tag="z")
-                mx_round(s)
+                    col = e * 4 + fb
+                    nc.scalar.activation(
+                        out=z[:, fb, :], in_=accs[fb][:], func=ACT.Gelu_apprx_sigmoid,
+                        bias=par["b"][:, col : col + 1], scale=1.0,
+                    )
+                for fb in range(4):
+                    col = e * 4 + fb
+                    eng = nc.vector if (s == NR - 1 and fb >= 2) else nc.gpsimd
+                    eng.tensor_scalar(
+                        out=z[:, fb, :], in0=z[:, fb, :],
+                        scalar1=par["s"][:, col : col + 1], scalar2=par["t"][:, col : col + 1],
+                        op0=ALU.mult, op1=ALU.add,
+                    )
             q = s + 1
             if 0 <= q < E:
                 nc.vector.quantize_mx(out=w_codes[q][:].bitcast(FP8X4), scales=w_scales[q][:], in_=grouped["w%d" % q][:])
@@ -218,32 +183,50 @@ def tile_mom_t_kernel(tc, x1, x2, x3, W, b, gamma, beta, running_mean, running_v
                 nc.vector.quantize_mx(out=c_t[:].bitcast(FP8X4), scales=s_t2[:], in_=grouped[q][:])
                 codes[q] = c_t
                 scales[q] = s_t2
+            if s == -1:
+                params_sqrt()
             a = s + 2
             if 0 <= a < E:
                 grouped["w%d" % a] = transposes_in(win[a], "w%d" % a, True)
             if 0 <= a < NR:
-                grouped[a] = transposes_in(xin[a], "x%d" % a, a < E)
+                grouped[a] = transposes_in(xin[a], "x%d" % a, a < 3)
             if s == -2:
-                params()
-            if has_back:
-                pair_a = back(o, (0, 1))
-                pair_b = back(o, (2, 3))
-                back_out(o, (0, 1), pair_a, on_scalar)
-                back_out(o, (2, 3), pair_b, on_scalar)
-            if s == NR - 1:
-                affine(nc.vector, s, 2)
-                affine(nc.vector, s, 3)
-
+                params_transpose()
+            if s == -1:
+                params_affine()
+            o = s - 1
+            if 0 <= o < NR:
+                tb, e = divmod(o, E)
+                if e == 0:
+                    stage[tb] = st_pool.tile([P, 4 * E * D], F32, name="st%d" % tb, tag="st")
+                banks = []
+                for jj in range(4):
+                    bank = psum.tile([P, D], F32, name="o%d_%d" % (o, jj), tag="bank")
+                    for fb in range(4):
+                        nc.tensor.transpose(bank[:, fb * P : (fb + 1) * P], zt[o][:, fb, jj * P : (jj + 1) * P], ident[:])
+                    banks.append(bank)
+                if o == NR - 1:
+                    on_scalar = (0, 2)
+                elif o % 2 == 1:
+                    on_scalar = (0, 1)
+                else:
+                    on_scalar = (0,)
+                for jj in range(4):
+                    dst = stage[tb][:, jj * E * D + e * D : jj * E * D + (e + 1) * D]
+                    if jj in on_scalar:
+                        nc.scalar.copy(out=dst, in_=banks[jj][:])
+                    else:
+                        nc.vector.tensor_copy(out=dst, in_=banks[jj][:])
             ld = s + PREFETCH
             if PREFETCH <= ld < NR:
                 load_x(ld)
-            if has_back:
+            if 0 <= o < NR:
                 tb, e = divmod(o, E)
                 if tb < TB - 1:
                     if e == E - 1:
                         store(tb, 0, 4, 0, E * D)
-                elif e == 1:
-                    store(tb, 0, 4, 0, 2 * D)
-                elif e == 2:
-                    store(tb, 0, 2, 2 * D, 3 * D)
-                    store(tb, 2, 4, 2 * D, 3 * D)
+                elif e < E - 1:
+                    store(tb, 0, 4, e * D, (e + 1) * D)
+                else:
+                    for jj in range(4):
+                        store(tb, jj, jj + 1, e * D, (e + 1) * D)

from contextlib import ExitStack

import concourse.mybir as mybir
from concourse.masks import make_identity

F32 = mybir.dt.float32
BF16 = mybir.dt.bfloat16
U32 = mybir.dt.uint32
U8 = mybir.dt.uint8
FP8X4 = mybir.dt.float8_e4m3fn_x4
ACT = mybir.ActivationFunctionType
ALU = mybir.AluOpType

P = 128
TOKENS = 4096
D = 512
E = 3
EPS = 1e-5
JT = TOKENS // P
TB = 8
NR = TB * E
FLOPS = 2 * TOKENS * D * D * E

X_BUFS = 20
PREFETCH = 16


def tile_mom_t_kernel(tc, x1, x2, x3, W, b, gamma, beta, running_mean, running_var, out):
    nc = tc.nc
    xs = [x.rearrange("(p j) k -> p (j k)", j=JT) for x in (x1, x2, x3)]
    w_rows = W.rearrange("o e f k -> (o e f) k")
    out_v = out.rearrange("(p j) c -> p j c", j=JT)

    with ExitStack() as ctx:
        const = ctx.enter_context(tc.tile_pool(name="const", bufs=1))
        xin_pool = ctx.enter_context(tc.tile_pool(name="xin", bufs=X_BUFS))
        grp_pool = ctx.enter_context(tc.tile_pool(name="grp", bufs=3))
        q_pool = ctx.enter_context(tc.tile_pool(name="q", bufs=3))
        z_pool = ctx.enter_context(tc.tile_pool(name="z", bufs=3))
        st_pool = ctx.enter_context(tc.tile_pool(name="st", bufs=3))
        psum = ctx.enter_context(tc.psum_pool(name="psum", bufs=8))
        ctx.enter_context(tc.manual_schedule())

        ident = const.tile([P, P], F32, name="ident")
        make_identity(nc, ident[:])

        prow = const.tile([P, P], BF16, name="prow")
        nc.vector.memset(prow[:], 0.0)
        for i, v in enumerate((b, gamma, beta, running_mean, running_var)):
            nc.scalar.dma_start(out=prow[16 * i : 16 * i + 12, :], in_=v.rearrange("o e (q c) -> (o e q) c", c=P))

        xin = {}
        win = {}

        def load_w(e):
            t = xin_pool.tile([P, 4 * D], BF16, name="win%d" % e, tag="xin")
            cuts = (0, 1, 2, 4) if e == 0 else (0, 4)
            for lo, hi in zip(cuts[:-1], cuts[1:]):
                nc.sync.dma_start(
                    out=t[:].rearrange("p (q k) -> p q k", q=4)[:, lo:hi, :],
                    in_=w_rows[e * D + lo * P : e * D + hi * P, :].rearrange("(q p) k -> p q k", p=P),
                )
            win[e] = t

        def load_x(r):
            tb, e = divmod(r, E)
            t = xin_pool.tile([P, 4 * D], BF16, name="xin%d" % r, tag="xin")
            cuts = (0, 2, 4) if r == 0 else (0, 4)
            for lo, hi in zip(cuts[:-1], cuts[1:]):
                nc.sync.dma_start(out=t[:, lo * D : hi * D], in_=xs[e][:, (tb * 4 + lo) * D : (tb * 4 + hi) * D])
            xin[r] = t

        for e in range(E):
            load_w(e)
            load_x(e)
        for r in range(E, PREFETCH):
            load_x(r)

        w_codes = [const.tile([P, D], U32, name="wc%d" % e, align_bytes=64) for e in range(E)]
        w_scales = [const.tile([P, D], U8, name="ws%d" % e, align_bytes=64) for e in range(E)]
        grouped = {}
        codes = {}
        scales = {}
        zt = {}
        stage = {}
        par = {}

        def transposes_in(src, key, on_scalar):
            sf = src[:].bitcast(F32)
            g = grp_pool.tile([P, 4 * D], BF16, name="g_%s" % key, tag="g", align_bytes=64)
            gf = g[:].bitcast(F32)
            banks = []
            for h in range(2):
                bank = psum.tile([P, D], F32, name="a_%s_%d" % (key, h), tag="bank")
                for jj in (2 * h, 2 * h + 1):
                    for u in range(2):
                        nc.tensor.transpose(
                            bank[:, u * 256 + (jj % 2) * P : u * 256 + (jj % 2) * P + P],
                            sf[:, jj * 256 + u * P : jj * 256 + u * P + P],
                            ident[:],
                        )
                banks.append(bank)
            for h in range(2):
                dst = gf[:, h * D : (h + 1) * D].rearrange("p (c u) -> p c u", u=2)
                srcv = banks[h][:].rearrange("p (u c) -> p c u", u=2)
                if h == 1 and on_scalar:
                    nc.scalar.copy(out=dst, in_=srcv)
                else:
                    nc.vector.tensor_copy(out=dst, in_=srcv)
            return g

        def params_transpose():
            pf = const.tile([P, P], F32, name="pf")
            nc.vector.tensor_copy(out=pf[:], in_=prow[:])
            bank = psum.tile([P, D], F32, name="pbank", tag="bank")
            nc.tensor.transpose(bank[:, 0:P], pf[:], ident[:])
            par["bank"] = bank

        def params_sqrt():
            pt = const.tile([P, P], F32, name="pt")
            nc.vector.tensor_copy(out=pt[:], in_=par["bank"][:, 0:P])
            sd = const.tile([P, 12], F32, name="sd")
            nc.vector.tensor_scalar_add(out=sd[:], in0=pt[:, 64:76], scalar1=EPS)
            nc.scalar.activation(out=sd[:], in_=sd[:], func=ACT.Sqrt)
            par["b"] = pt
            par["sd"] = sd

        def params_affine():
            pt = par["b"]
            s_t = const.tile([P, 12], F32, name="s_t")
            nc.vector.reciprocal(out=s_t[:], in_=par["sd"][:])
            nc.vector.tensor_mul(out=s_t[:], in0=s_t[:], in1=pt[:, 16:28])
            t_t = const.tile([P, 12], F32, name="t_t")
            nc.vector.tensor_mul(out=t_t[:], in0=pt[:, 48:60], in1=s_t[:])
            nc.vector.tensor_sub(out=t_t[:], in0=pt[:, 32:44], in1=t_t[:])
            par["s"] = s_t
            par["t"] = t_t

        def store(tb, lo, hi, c0, c1):
            nc.sync.dma_start(
                out=out_v[:, tb * 4 + lo : tb * 4 + hi, c0:c1],
                in_=stage[tb][:].rearrange("p (j c) -> p j c", j=4)[:, lo:hi, c0:c1],
            )

        for s in range(-2, NR + 1):
            if 0 <= s < NR:
                e = s % E
                z = z_pool.tile([P, 4, D], F32, name="z%d" % s, tag="z")
                zt[s] = z
                accs = []
                for fb in range(4):
                    acc = psum.tile([P, D], F32, name="acc%d_%d" % (s, fb), tag="bank")
                    nc.tensor.matmul_mx(
                        out=acc[:],
                        lhsT=w_codes[e][:, fb * P : (fb + 1) * P].bitcast(FP8X4),
                        lhsT_scale=w_scales[e][:, fb * P : (fb + 1) * P],
                        rhs=codes[s][:].bitcast(FP8X4),
                        rhs_scale=scales[s][:],
                        start=True,
                        stop=True,
                    )
                    accs.append(acc)
                for fb in range(4):
                    col = e * 4 + fb
                    nc.scalar.activation(
                        out=z[:, fb, :], in_=accs[fb][:], func=ACT.Gelu_apprx_sigmoid,
                        bias=par["b"][:, col : col + 1], scale=1.0,
                    )
                for fb in range(4):
                    col = e * 4 + fb
                    eng = nc.vector if (s == NR - 1 and fb >= 2) else nc.gpsimd
                    eng.tensor_scalar(
                        out=z[:, fb, :], in0=z[:, fb, :],
                        scalar1=par["s"][:, col : col + 1], scalar2=par["t"][:, col : col + 1],
                        op0=ALU.mult, op1=ALU.add,
                    )
            q = s + 1
            if 0 <= q < E:
                nc.vector.quantize_mx(out=w_codes[q][:].bitcast(FP8X4), scales=w_scales[q][:], in_=grouped["w%d" % q][:])
            if 0 <= q < NR:
                c_t = q_pool.tile([P, D], U32, name="c%d" % q, tag="c", align_bytes=64)
                s_t2 = q_pool.tile([P, D], U8, name="s%d" % q, tag="s", align_bytes=64)
                nc.vector.quantize_mx(out=c_t[:].bitcast(FP8X4), scales=s_t2[:], in_=grouped[q][:])
                codes[q] = c_t
                scales[q] = s_t2
            if s == -1:
                params_sqrt()
            a = s + 2
            if 0 <= a < E:
                grouped["w%d" % a] = transposes_in(win[a], "w%d" % a, True)
            if 0 <= a < NR:
                grouped[a] = transposes_in(xin[a], "x%d" % a, a < 3)
            if s == -2:
                params_transpose()
            if s == -1:
                params_affine()
            o = s - 1
            if 0 <= o < NR:
                tb, e = divmod(o, E)
                if e == 0:
                    stage[tb] = st_pool.tile([P, 4 * E * D], F32, name="st%d" % tb, tag="st")
                banks = []
                for jj in range(4):
                    bank = psum.tile([P, D], F32, name="o%d_%d" % (o, jj), tag="bank")
                    for fb in range(4):
                        nc.tensor.transpose(bank[:, fb * P : (fb + 1) * P], zt[o][:, fb, jj * P : (jj + 1) * P], ident[:])
                    banks.append(bank)
                if o == NR - 1:
                    on_scalar = (0, 2)
                elif o % 2 == 1:
                    on_scalar = (0, 1)
                else:
                    on_scalar = (0,)
                for jj in range(4):
                    dst = stage[tb][:, jj * E * D + e * D : jj * E * D + (e + 1) * D]
                    if jj in on_scalar:
                        nc.scalar.copy(out=dst, in_=banks[jj][:])
                    else:
                        nc.vector.tensor_copy(out=dst, in_=banks[jj][:])
            ld = s + PREFETCH
            if PREFETCH <= ld < NR:
                load_x(ld)
            if 0 <= o < NR:
                tb, e = divmod(o, E)
                if tb < TB - 1:
                    if e == E - 1:
                        store(tb, 0, 4, 0, E * D)
                elif e < E - 1:
                    store(tb, 0, 4, e * D, (e + 1) * D)
                else:
                    for jj in range(4):
                        store(tb, jj, jj + 1, e * D, (e + 1) * D)
